import numpy as np
import ml_dtypes

BF16 = ml_dtypes.bfloat16


def bf(x):
    return np.asarray(x, np.float32).astype(BF16)


def f32(x):
    return np.asarray(x, np.float32)


def f64(x):
    return np.asarray(x).astype(np.float64)


def striped(idx):
    return np.tile(idx.reshape(-1, 16).T, (8, 1))


HID, H, D, C, S, N = 512, 4, 128, 512, 1024, 512
EPS = 1e-6


def setup_inputs():
    return {"x": bf(np.random.standard_normal((HID, N))), "wk": bf(np.random.standard_normal((HID, C)) / np.sqrt(HID)), "w": f32(0.1 * np.random.standard_normal((D, 1))), "base": f32(np.random.standard_normal((C, S))), "offs": striped(np.random.permutation(S)[:N])}


def reference(x, wk, w, base, offs):
    idx = offs[:16].T.reshape(-1)
    kp = (f64(wk).T @ f64(x)).reshape(H, D, N)
    r = 1.0 / np.sqrt(np.mean(kp * kp, axis=1, keepdims=True) + EPS)
    res = f64(base).copy()
    res[:, idx] = ((kp * (1.0 + f64(w))[None, :, :]) * r).reshape(C, N)
    return res

@@ -1,0 +1,68 @@
+import concourse.mybir as mybir
+
+BF16, F32, U16 = mybir.dt.bfloat16, mybir.dt.float32, mybir.dt.uint16
+ACT = mybir.ActivationFunctionType
+MULT = mybir.AluOpType.mult
+
+P = 128
+HID = 512
+HEADS = 4
+TOKENS = 512
+PLACES = 1024
+HID_BLOCKS = HID // P
+EPS = 1e-6
+
+FLOPS = 2 * HID * HEADS * P * TOKENS
+
+
+def tile_fullattention_kernel(tc, x, wk, w, base, offs, out):
+    nc = tc.nc
+    with (
+        tc.tile_pool(name="held", bufs=1) as held,
+        tc.tile_pool(name="work", bufs=2) as work,
+        tc.psum_pool(name="kp_banks", bufs=HEADS) as kp_banks,
+        tc.psum_pool(name="mean_banks", bufs=2) as mean_banks,
+    ):
+        offsets = held.tile([P, TOKENS // 16], U16, name="offsets")
+        nc.sync.dma_start(offsets[:], offs)
+
+        x_blocks = [held.tile([P, TOKENS], BF16, name=f"x{k}") for k in range(HID_BLOCKS)]
+        wk_blocks = [held.tile([P, HEADS * P], BF16, name=f"wk{k}") for k in range(HID_BLOCKS)]
+        for k in range(HID_BLOCKS):
+            nc.sync.dma_start(x_blocks[k][:], x[k * P : (k + 1) * P, :])
+            nc.scalar.dma_start(wk_blocks[k][:], wk[k * P : (k + 1) * P, :])
+        w_column = held.tile([P, 1], F32, name="w_column")
+        nc.scalar.dma_start(w_column[:], w)
+
+        windows = [held.tile([P, PLACES], F32, name=f"window{h}") for h in range(HEADS)]
+        for h in range(HEADS):
+            nc.sync.dma_start(windows[h][:], base[h * P : (h + 1) * P, :])
+
+        gain = held.tile([P, 1], F32, name="gain")
+        nc.vector.tensor_scalar_add(gain[:], w_column[:], 1.0)
+        eps = held.tile([P, 1], F32, name="eps")
+        nc.vector.memset(eps[:], EPS)
+        averager = held.tile([P, P], BF16, name="averager")
+        nc.vector.memset(averager[:], 1.0 / P)
+
+        for h in range(HEADS):
+            kp = kp_banks.tile([P, TOKENS], F32, name="kp")
+            for k in range(HID_BLOCKS):
+                nc.tensor.matmul(
+                    kp[:],
+                    wk_blocks[k][:, h * P : (h + 1) * P],
+                    x_blocks[k][:],
+                    start=(k == 0),
+                    stop=(k == HID_BLOCKS - 1),
+                )
+            squares = work.tile([P, TOKENS], BF16, name="squares")
+            nc.scalar.activation(squares[:], kp[:], ACT.Square)
+            mean_square = mean_banks.tile([P, TOKENS], F32, name="mean_square")
+            nc.tensor.matmul(mean_square[:], averager[:], squares[:], start=True, stop=True)
+            gained = work.tile([P, TOKENS], F32, name="gained")
+            nc.scalar.activation(gained[:], kp[:], ACT.Identity, scale=gain[:])
+            r = work.tile([P, TOKENS], F32, name="r")
+            nc.scalar.activation(r[:], mean_square[:], ACT.Abs_reciprocal_sqrt, bias=eps[:])
+
+            nc.vector.tensor_tensor(windows[h][:].indirect(offsets[:]), gained[:], r[:], MULT)
+            nc.sync.dma_start(out[h * P : (h + 1) * P, :], windows[h][:])

@@ -42,6 +42,8 @@ def tile_fullattention_kernel(tc, x, wk, w, base, offs, out):
         nc.vector.tensor_scalar_add(gain[:], w_column[:], 1.0)
         eps = held.tile([P, 1], F32, name="eps")
         nc.vector.memset(eps[:], EPS)
+        table_warmer = held.tile([P, 1], F32, name="table_warmer")
+        nc.scalar.activation(table_warmer[:], eps[:], ACT.Abs_reciprocal_sqrt)
         averager = held.tile([P, P], BF16, name="averager")
         nc.vector.memset(averager[:], 1.0 / P)
 

@@ -10,6 +10,8 @@ HEADS = 4
 TOKENS = 512
 PLACES = 1024
 HID_BLOCKS = HID // P
+PIECE = 256
+PIECES = TOKENS // PIECE
 EPS = 1e-6
 
 FLOPS = 2 * HID * HEADS * P * TOKENS
@@ -19,52 +21,59 @@ def tile_fullattention_kernel(tc, x, wk, w, base, offs, out):
     nc = tc.nc
     with (
         tc.tile_pool(name="held", bufs=1) as held,
-        tc.tile_pool(name="work", bufs=2) as work,
-        tc.psum_pool(name="kp_banks", bufs=HEADS) as kp_banks,
+        tc.tile_pool(name="work", bufs=3) as work,
+        tc.psum_pool(name="kp_banks", bufs=3) as kp_banks,
         tc.psum_pool(name="mean_banks", bufs=2) as mean_banks,
     ):
-        offsets = held.tile([P, TOKENS // 16], U16, name="offsets")
-        nc.sync.dma_start(offsets[:], offs)
-
-        x_blocks = [held.tile([P, TOKENS], BF16, name=f"x{k}") for k in range(HID_BLOCKS)]
-        wk_blocks = [held.tile([P, HEADS * P], BF16, name=f"wk{k}") for k in range(HID_BLOCKS)]
-        for k in range(HID_BLOCKS):
-            nc.sync.dma_start(x_blocks[k][:], x[k * P : (k + 1) * P, :])
-            nc.scalar.dma_start(wk_blocks[k][:], wk[k * P : (k + 1) * P, :])
+        x_rows = held.tile([P, HID_BLOCKS, TOKENS], BF16, name="x_rows")
+        nc.sync.dma_start(x_rows[:], x.rearrange("(p k) j -> p k j", k=HID_BLOCKS))
+        wk_rows = held.tile([P, HID_BLOCKS, HEADS * P], BF16, name="wk_rows")
+        nc.scalar.dma_start(wk_rows[:], wk.rearrange("(p k) c -> p k c", k=HID_BLOCKS))
         w_column = held.tile([P, 1], F32, name="w_column")
         nc.scalar.dma_start(w_column[:], w)
-
+        offsets = held.tile([P, TOKENS // 16], U16, name="offsets")
+        nc.sync.dma_start(offsets[:], offs)
         windows = [held.tile([P, PLACES], F32, name=f"window{h}") for h in range(HEADS)]
         for h in range(HEADS):
             nc.sync.dma_start(windows[h][:], base[h * P : (h + 1) * P, :])
 
-        gain = held.tile([P, 1], F32, name="gain")
-        nc.vector.tensor_scalar_add(gain[:], w_column[:], 1.0)
         eps = held.tile([P, 1], F32, name="eps")
         nc.vector.memset(eps[:], EPS)
         table_warmer = held.tile([P, 1], F32, name="table_warmer")
         nc.scalar.activation(table_warmer[:], eps[:], ACT.Abs_reciprocal_sqrt)
         averager = held.tile([P, P], BF16, name="averager")
         nc.vector.memset(averager[:], 1.0 / P)
+        gain = held.tile([P, 1], F32, name="gain")
+        nc.vector.tensor_scalar_add(gain[:], w_column[:], 1.0)
 
-        for h in range(HEADS):
-            kp = kp_banks.tile([P, TOKENS], F32, name="kp")
+        def project(h, t):
+            kp = kp_banks.tile([P, PIECE], F32, name="kp")
             for k in range(HID_BLOCKS):
                 nc.tensor.matmul(
                     kp[:],
-                    wk_blocks[k][:, h * P : (h + 1) * P],
-                    x_blocks[k][:],
+                    wk_rows[:, k, h * P : (h + 1) * P],
+                    x_rows[:, k, t * PIECE : (t + 1) * PIECE],
                     start=(k == 0),
                     stop=(k == HID_BLOCKS - 1),
                 )
-            squares = work.tile([P, TOKENS], BF16, name="squares")
+            squares = work.tile([P, PIECE], BF16, name="squares")
             nc.scalar.activation(squares[:], kp[:], ACT.Square)
-            mean_square = mean_banks.tile([P, TOKENS], F32, name="mean_square")
-            nc.tensor.matmul(mean_square[:], averager[:], squares[:], start=True, stop=True)
-            gained = work.tile([P, TOKENS], F32, name="gained")
+            return kp, squares
+
+        pieces = [(h, t) for h in range(HEADS) for t in range(PIECES)]
+        ahead = project(*pieces[0])
+        for i, (h, t) in enumerate(pieces):
+            kp, squares = ahead
+            gained = work.tile([P, PIECE], F32, name="gained")
             nc.scalar.activation(gained[:], kp[:], ACT.Identity, scale=gain[:])
-            r = work.tile([P, TOKENS], F32, name="r")
+            if i + 1 < len(pieces):
+                ahead = project(*pieces[i + 1])
+            mean_square = mean_banks.tile([P, PIECE], F32, name="mean_square")
+            nc.tensor.matmul(mean_square[:], averager[:], squares[:], start=True, stop=True)
+            r = work.tile([P, PIECE], F32, name="r")
             nc.scalar.activation(r[:], mean_square[:], ACT.Abs_reciprocal_sqrt, bias=eps[:])
 
-            nc.vector.tensor_tensor(windows[h][:].indirect(offsets[:]), gained[:], r[:], MULT)
-            nc.sync.dma_start(out[h * P : (h + 1) * P, :], windows[h][:])
+            piece_offsets = offsets[:, t * PIECE // 16 : (t + 1) * PIECE // 16]
+            nc.vector.tensor_tensor(windows[h][:].indirect(piece_offsets), gained[:], r[:], MULT)
+            if t == PIECES - 1:
+                nc.sync.dma_start(out[h * P : (h + 1) * P, :], windows[h][:])

@@ -19,22 +19,28 @@ FLOPS = 2 * HID * HEADS * P * TOKENS
 
 def tile_fullattention_kernel(tc, x, wk, w, base, offs, out):
     nc = tc.nc
+    x_view = x.rearrange("(k p) j -> p k j", p=P)
+    wk_view = wk.rearrange("(k p) c -> p k c", p=P)
     with (
         tc.tile_pool(name="held", bufs=1) as held,
         tc.tile_pool(name="work", bufs=3) as work,
         tc.psum_pool(name="kp_banks", bufs=3) as kp_banks,
         tc.psum_pool(name="mean_banks", bufs=2) as mean_banks,
     ):
-        x_rows = held.tile([P, HID_BLOCKS, TOKENS], BF16, name="x_rows")
-        nc.sync.dma_start(x_rows[:], x.rearrange("(p k) j -> p k j", k=HID_BLOCKS))
-        wk_rows = held.tile([P, HID_BLOCKS, HEADS * P], BF16, name="wk_rows")
-        nc.scalar.dma_start(wk_rows[:], wk.rearrange("(p k) c -> p k c", k=HID_BLOCKS))
-        w_column = held.tile([P, 1], F32, name="w_column")
-        nc.scalar.dma_start(w_column[:], w)
-        offsets = held.tile([P, TOKENS // 16], U16, name="offsets")
-        nc.sync.dma_start(offsets[:], offs)
+        x_pieces = [held.tile([P, HID_BLOCKS, PIECE], BF16, name=f"x_piece{t}") for t in range(PIECES)]
+        wk_heads = [held.tile([P, HID_BLOCKS, P], BF16, name=f"wk_head{h}") for h in range(HEADS)]
         windows = [held.tile([P, PLACES], F32, name=f"window{h}") for h in range(HEADS)]
-        for h in range(HEADS):
+        offsets = held.tile([P, TOKENS // 16], U16, name="offsets")
+        w_column = held.tile([P, 1], F32, name="w_column")
+
+        nc.scalar.dma_start(w_column[:], w)
+        nc.sync.dma_start(wk_heads[0][:], wk_view[:, :, 0:P])
+        for t in range(PIECES):
+            nc.sync.dma_start(x_pieces[t][:], x_view[:, :, t * PIECE : (t + 1) * PIECE])
+        nc.sync.dma_start(offsets[:], offs)
+        nc.sync.dma_start(windows[0][:], base[0:P, :])
+        for h in range(1, HEADS):
+            nc.sync.dma_start(wk_heads[h][:], wk_view[:, :, h * P : (h + 1) * P])
             nc.sync.dma_start(windows[h][:], base[h * P : (h + 1) * P, :])
 
         eps = held.tile([P, 1], F32, name="eps")
@@ -51,8 +57,8 @@ def tile_fullattention_kernel(tc, x, wk, w, base, offs, out):
             for k in range(HID_BLOCKS):
                 nc.tensor.matmul(
                     kp[:],
-                    wk_rows[:, k, h * P : (h + 1) * P],
-                    x_rows[:, k, t * PIECE : (t + 1) * PIECE],
+                    wk_heads[h][:, k, :],
+                    x_pieces[t][:, k, :],
                     start=(k == 0),
                     stop=(k == HID_BLOCKS - 1),
                 )

@@ -13,6 +13,7 @@ HID_BLOCKS = HID // P
 PIECE = 256
 PIECES = TOKENS // PIECE
 EPS = 1e-6
+PAIR = 2
 
 FLOPS = 2 * HID * HEADS * P * TOKENS
 
@@ -35,12 +36,16 @@ def tile_fullattention_kernel(tc, x, wk, w, base, offs, out):
 
         nc.scalar.dma_start(w_column[:], w)
         nc.sync.dma_start(wk_heads[0][:], wk_view[:, :, 0:P])
-        for t in range(PIECES):
+        nc.sync.dma_start(x_pieces[0][:], x_view[:, :, 0:PIECE])
+        nc.sync.dma_start(wk_heads[1][:], wk_view[:, :, P : 2 * P])
+        for t in range(1, PIECES):
             nc.sync.dma_start(x_pieces[t][:], x_view[:, :, t * PIECE : (t + 1) * PIECE])
         nc.sync.dma_start(offsets[:], offs)
         nc.sync.dma_start(windows[0][:], base[0:P, :])
-        for h in range(1, HEADS):
+        nc.sync.dma_start(windows[1][:], base[P : 2 * P, :])
+        for h in range(PAIR, HEADS):
             nc.sync.dma_start(wk_heads[h][:], wk_view[:, :, h * P : (h + 1) * P])
+        for h in range(PAIR, HEADS):
             nc.sync.dma_start(windows[h][:], base[h * P : (h + 1) * P, :])
 
         eps = held.tile([P, 1], F32, name="eps")
@@ -52,34 +57,28 @@ def tile_fullattention_kernel(tc, x, wk, w, base, offs, out):
         gain = held.tile([P, 1], F32, name="gain")
         nc.vector.tensor_scalar_add(gain[:], w_column[:], 1.0)
 
-        def project(h, t):
-            kp = kp_banks.tile([P, PIECE], F32, name="kp")
-            for k in range(HID_BLOCKS):
-                nc.tensor.matmul(
-                    kp[:],
-                    wk_heads[h][:, k, :],
-                    x_pieces[t][:, k, :],
-                    start=(k == 0),
-                    stop=(k == HID_BLOCKS - 1),
-                )
-            squares = work.tile([P, PIECE], BF16, name="squares")
-            nc.scalar.activation(squares[:], kp[:], ACT.Square)
-            return kp, squares
+        for first_head in range(0, HEADS, PAIR):
+            for t in range(PIECES):
+                for h in range(first_head, first_head + PAIR):
+                    kp = kp_banks.tile([P, PIECE], F32, name="kp")
+                    for k in range(HID_BLOCKS):
+                        nc.tensor.matmul(
+                            kp[:],
+                            wk_heads[h][:, k, :],
+                            x_pieces[t][:, k, :],
+                            start=(k == 0),
+                            stop=(k == HID_BLOCKS - 1),
+                        )
+                    squares = work.tile([P, PIECE], BF16, name="squares")
+                    nc.scalar.activation(squares[:], kp[:], ACT.Square)
+                    mean_square = mean_banks.tile([P, PIECE], F32, name="mean_square")
+                    nc.tensor.matmul(mean_square[:], averager[:], squares[:], start=True, stop=True)
+                    gained = work.tile([P, PIECE], F32, name="gained")
+                    nc.scalar.activation(gained[:], kp[:], ACT.Identity, scale=gain[:])
+                    r = work.tile([P, PIECE], F32, name="r")
+                    nc.scalar.activation(r[:], mean_square[:], ACT.Abs_reciprocal_sqrt, bias=eps[:])
 
-        pieces = [(h, t) for h in range(HEADS) for t in range(PIECES)]
-        ahead = project(*pieces[0])
-        for i, (h, t) in enumerate(pieces):
-            kp, squares = ahead
-            gained = work.tile([P, PIECE], F32, name="gained")
-            nc.scalar.activation(gained[:], kp[:], ACT.Identity, scale=gain[:])
-            if i + 1 < len(pieces):
-                ahead = project(*pieces[i + 1])
-            mean_square = mean_banks.tile([P, PIECE], F32, name="mean_square")
-            nc.tensor.matmul(mean_square[:], averager[:], squares[:], start=True, stop=True)
-            r = work.tile([P, PIECE], F32, name="r")
-            nc.scalar.activation(r[:], mean_square[:], ACT.Abs_reciprocal_sqrt, bias=eps[:])
-
-            piece_offsets = offsets[:, t * PIECE // 16 : (t + 1) * PIECE // 16]
-            nc.vector.tensor_tensor(windows[h][:].indirect(piece_offsets), gained[:], r[:], MULT)
-            if t == PIECES - 1:
-                nc.sync.dma_start(out[h * P : (h + 1) * P, :], windows[h][:])
+                    piece_offsets = offsets[:, t * PIECE // 16 : (t + 1) * PIECE // 16]
+                    nc.vector.tensor_tensor(windows[h][:].indirect(piece_offsets), gained[:], r[:], MULT)
+                    if t == PIECES - 1:
+                        nc.sync.dma_start(out[h * P : (h + 1) * P, :], windows[h][:])

@@ -34,15 +34,14 @@ def tile_fullattention_kernel(tc, x, wk, w, base, offs, out):
         offsets = held.tile([P, TOKENS // 16], U16, name="offsets")
         w_column = held.tile([P, 1], F32, name="w_column")
 
-        nc.scalar.dma_start(w_column[:], w)
         nc.sync.dma_start(wk_heads[0][:], wk_view[:, :, 0:P])
-        nc.sync.dma_start(x_pieces[0][:], x_view[:, :, 0:PIECE])
-        nc.sync.dma_start(wk_heads[1][:], wk_view[:, :, P : 2 * P])
-        for t in range(1, PIECES):
+        nc.scalar.dma_start(wk_heads[1][:], wk_view[:, :, P : 2 * P])
+        nc.scalar.dma_start(w_column[:], w)
+        for t in range(PIECES):
             nc.sync.dma_start(x_pieces[t][:], x_view[:, :, t * PIECE : (t + 1) * PIECE])
         nc.sync.dma_start(offsets[:], offs)
-        nc.sync.dma_start(windows[0][:], base[0:P, :])
-        nc.sync.dma_start(windows[1][:], base[P : 2 * P, :])
+        for h in range(PAIR):
+            nc.sync.dma_start(windows[h][:], base[h * P : (h + 1) * P, :])
         for h in range(PAIR, HEADS):
             nc.sync.dma_start(wk_heads[h][:], wk_view[:, :, h * P : (h + 1) * P])
         for h in range(PAIR, HEADS):

@@ -14,6 +14,7 @@ PIECE = 256
 PIECES = TOKENS // PIECE
 EPS = 1e-6
 PAIR = 2
+PE_WARMERS = 10
 
 FLOPS = 2 * HID * HEADS * P * TOKENS
 
@@ -27,6 +28,7 @@ def tile_fullattention_kernel(tc, x, wk, w, base, offs, out):
         tc.tile_pool(name="work", bufs=3) as work,
         tc.psum_pool(name="kp_banks", bufs=3) as kp_banks,
         tc.psum_pool(name="mean_banks", bufs=2) as mean_banks,
+        tc.psum_pool(name="idle_banks", bufs=1) as idle_banks,
     ):
         x_pieces = [held.tile([P, HID_BLOCKS, PIECE], BF16, name=f"x_piece{t}") for t in range(PIECES)]
         wk_heads = [held.tile([P, HID_BLOCKS, P], BF16, name=f"wk_head{h}") for h in range(HEADS)]
@@ -34,14 +36,15 @@ def tile_fullattention_kernel(tc, x, wk, w, base, offs, out):
         offsets = held.tile([P, TOKENS // 16], U16, name="offsets")
         w_column = held.tile([P, 1], F32, name="w_column")
 
-        nc.sync.dma_start(wk_heads[0][:], wk_view[:, :, 0:P])
-        nc.scalar.dma_start(wk_heads[1][:], wk_view[:, :, P : 2 * P])
         nc.scalar.dma_start(w_column[:], w)
-        for t in range(PIECES):
+        nc.sync.dma_start(wk_heads[0][:], wk_view[:, :, 0:P])
+        nc.sync.dma_start(x_pieces[0][:], x_view[:, :, 0:PIECE])
+        nc.sync.dma_start(wk_heads[1][:], wk_view[:, :, P : 2 * P])
+        for t in range(1, PIECES):
             nc.sync.dma_start(x_pieces[t][:], x_view[:, :, t * PIECE : (t + 1) * PIECE])
         nc.sync.dma_start(offsets[:], offs)
-        for h in range(PAIR):
-            nc.sync.dma_start(windows[h][:], base[h * P : (h + 1) * P, :])
+        nc.sync.dma_start(windows[0][:], base[0:P, :])
+        nc.sync.dma_start(windows[1][:], base[P : 2 * P, :])
         for h in range(PAIR, HEADS):
             nc.sync.dma_start(wk_heads[h][:], wk_view[:, :, h * P : (h + 1) * P])
         for h in range(PAIR, HEADS):
@@ -53,6 +56,11 @@ def tile_fullattention_kernel(tc, x, wk, w, base, offs, out):
         nc.scalar.activation(table_warmer[:], eps[:], ACT.Abs_reciprocal_sqrt)
         averager = held.tile([P, P], BF16, name="averager")
         nc.vector.memset(averager[:], 1.0 / P)
+
+        idle_product = idle_banks.tile([P, P], F32, name="idle_product")
+        for i in range(PE_WARMERS):
+            nc.tensor.matmul(idle_product[:], averager[:], averager[:], start=True, stop=True)
+
         gain = held.tile([P, 1], F32, name="gain")
         nc.vector.tensor_scalar_add(gain[:], w_column[:], 1.0)
 

@@ -14,7 +14,7 @@ PIECE = 256
 PIECES = TOKENS // PIECE
 EPS = 1e-6
 PAIR = 2
-PE_WARMERS = 10
+PE_WARMERS = 4
 
 FLOPS = 2 * HID * HEADS * P * TOKENS
 
@@ -54,12 +54,13 @@ def tile_fullattention_kernel(tc, x, wk, w, base, offs, out):
         nc.vector.memset(eps[:], EPS)
         table_warmer = held.tile([P, 1], F32, name="table_warmer")
         nc.scalar.activation(table_warmer[:], eps[:], ACT.Abs_reciprocal_sqrt)
-        averager = held.tile([P, P], BF16, name="averager")
-        nc.vector.memset(averager[:], 1.0 / P)
+        fractions = held.tile([P, TOKENS], BF16, name="fractions")
+        nc.vector.memset(fractions[:], 1.0 / P)
+        averager = fractions[:, 0:P]
 
-        idle_product = idle_banks.tile([P, P], F32, name="idle_product")
+        idle_product = idle_banks.tile([P, TOKENS], F32, name="idle_product")
         for i in range(PE_WARMERS):
-            nc.tensor.matmul(idle_product[:], averager[:], averager[:], start=True, stop=True)
+            nc.tensor.matmul(idle_product[:], averager, fractions[:], start=True, stop=True)
 
         gain = held.tile([P, 1], F32, name="gain")
         nc.vector.tensor_scalar_add(gain[:], w_column[:], 1.0)
@@ -79,7 +80,7 @@ def tile_fullattention_kernel(tc, x, wk, w, base, offs, out):
                     squares = work.tile([P, PIECE], BF16, name="squares")
                     nc.scalar.activation(squares[:], kp[:], ACT.Square)
                     mean_square = mean_banks.tile([P, PIECE], F32, name="mean_square")
-                    nc.tensor.matmul(mean_square[:], averager[:], squares[:], start=True, stop=True)
+                    nc.tensor.matmul(mean_square[:], averager, squares[:], start=True, stop=True)
                     gained = work.tile([P, PIECE], F32, name="gained")
                     nc.scalar.activation(gained[:], kp[:], ACT.Identity, scale=gain[:])
                     r = work.tile([P, PIECE], F32, name="r")

@@ -39,12 +39,12 @@ def tile_fullattention_kernel(tc, x, wk, w, base, offs, out):
         nc.scalar.dma_start(w_column[:], w)
         nc.sync.dma_start(wk_heads[0][:], wk_view[:, :, 0:P])
         nc.sync.dma_start(x_pieces[0][:], x_view[:, :, 0:PIECE])
-        nc.sync.dma_start(wk_heads[1][:], wk_view[:, :, P : 2 * P])
-        for t in range(1, PIECES):
-            nc.sync.dma_start(x_pieces[t][:], x_view[:, :, t * PIECE : (t + 1) * PIECE])
         nc.sync.dma_start(offsets[:], offs)
         nc.sync.dma_start(windows[0][:], base[0:P, :])
+        nc.sync.dma_start(wk_heads[1][:], wk_view[:, :, P : 2 * P])
         nc.sync.dma_start(windows[1][:], base[P : 2 * P, :])
+        for t in range(1, PIECES):
+            nc.sync.dma_start(x_pieces[t][:], x_view[:, :, t * PIECE : (t + 1) * PIECE])
         for h in range(PAIR, HEADS):
             nc.sync.dma_start(wk_heads[h][:], wk_view[:, :, h * P : (h + 1) * P])
         for h in range(PAIR, HEADS):

@@ -65,28 +65,36 @@ def tile_fullattention_kernel(tc, x, wk, w, base, offs, out):
         gain = held.tile([P, 1], F32, name="gain")
         nc.vector.tensor_scalar_add(gain[:], w_column[:], 1.0)
 
-        for first_head in range(0, HEADS, PAIR):
-            for t in range(PIECES):
-                for h in range(first_head, first_head + PAIR):
-                    kp = kp_banks.tile([P, PIECE], F32, name="kp")
-                    for k in range(HID_BLOCKS):
-                        nc.tensor.matmul(
-                            kp[:],
-                            wk_heads[h][:, k, :],
-                            x_pieces[t][:, k, :],
-                            start=(k == 0),
-                            stop=(k == HID_BLOCKS - 1),
-                        )
-                    squares = work.tile([P, PIECE], BF16, name="squares")
-                    nc.scalar.activation(squares[:], kp[:], ACT.Square)
-                    mean_square = mean_banks.tile([P, PIECE], F32, name="mean_square")
-                    nc.tensor.matmul(mean_square[:], averager, squares[:], start=True, stop=True)
-                    gained = work.tile([P, PIECE], F32, name="gained")
-                    nc.scalar.activation(gained[:], kp[:], ACT.Identity, scale=gain[:])
-                    r = work.tile([P, PIECE], F32, name="r")
-                    nc.scalar.activation(r[:], mean_square[:], ACT.Abs_reciprocal_sqrt, bias=eps[:])
+        def project_normalise_scatter(h, first_piece, pieces):
+            tokens = pieces * PIECE
+            kp = kp_banks.tile([P, TOKENS], F32, name="kp")
+            for i in range(pieces):
+                for k in range(HID_BLOCKS):
+                    nc.tensor.matmul(
+                        kp[:, i * PIECE : (i + 1) * PIECE],
+                        wk_heads[h][:, k, :],
+                        x_pieces[first_piece + i][:, k, :],
+                        start=(k == 0),
+                        stop=(k == HID_BLOCKS - 1),
+                    )
+            squares = work.tile([P, TOKENS], BF16, name="squares")
+            nc.scalar.activation(squares[:, 0:tokens], kp[:, 0:tokens], ACT.Square)
+            mean_square = mean_banks.tile([P, TOKENS], F32, name="mean_square")
+            nc.tensor.matmul(mean_square[:, 0:tokens], averager, squares[:, 0:tokens], start=True, stop=True)
+            gained = work.tile([P, TOKENS], F32, name="gained")
+            nc.scalar.activation(gained[:, 0:tokens], kp[:, 0:tokens], ACT.Identity, scale=gain[:])
+            r = work.tile([P, TOKENS], F32, name="r")
+            nc.scalar.activation(r[:, 0:tokens], mean_square[:, 0:tokens], ACT.Abs_reciprocal_sqrt, bias=eps[:])
 
-                    piece_offsets = offsets[:, t * PIECE // 16 : (t + 1) * PIECE // 16]
-                    nc.vector.tensor_tensor(windows[h][:].indirect(piece_offsets), gained[:], r[:], MULT)
-                    if t == PIECES - 1:
-                        nc.sync.dma_start(out[h * P : (h + 1) * P, :], windows[h][:])
+            first_column = first_piece * PIECE // 16
+            piece_offsets = offsets[:, first_column : first_column + tokens // 16]
+            nc.vector.tensor_tensor(windows[h][:].indirect(piece_offsets), gained[:, 0:tokens], r[:, 0:tokens], MULT)
+
+        for t in range(PIECES):
+            for h in range(PAIR):
+                project_normalise_scatter(h, t, 1)
+        for h in range(PAIR):
+            nc.sync.dma_start(out[h * P : (h + 1) * P, :], windows[h][:])
+        for h in range(PAIR, HEADS):
+            project_normalise_scatter(h, 0, PIECES)
+            nc.sync.dma_start(out[h * P : (h + 1) * P, :], windows[h][:])

@@ -10,10 +10,9 @@ HEADS = 4
 TOKENS = 512
 PLACES = 1024
 HID_BLOCKS = HID // P
-PIECE = 256
-PIECES = TOKENS // PIECE
 EPS = 1e-6
 PAIR = 2
+PIECE = 256
 PE_WARMERS = 4
 
 FLOPS = 2 * HID * HEADS * P * TOKENS
@@ -30,25 +29,33 @@ def tile_fullattention_kernel(tc, x, wk, w, base, offs, out):
         tc.psum_pool(name="mean_banks", bufs=2) as mean_banks,
         tc.psum_pool(name="idle_banks", bufs=1) as idle_banks,
     ):
-        x_pieces = [held.tile([P, HID_BLOCKS, PIECE], BF16, name=f"x_piece{t}") for t in range(PIECES)]
+        x_all = held.tile([P, HID_BLOCKS, TOKENS], BF16, name="x_all")
         wk_heads = [held.tile([P, HID_BLOCKS, P], BF16, name=f"wk_head{h}") for h in range(HEADS)]
         windows = [held.tile([P, PLACES], F32, name=f"window{h}") for h in range(HEADS)]
         offsets = held.tile([P, TOKENS // 16], U16, name="offsets")
         w_column = held.tile([P, 1], F32, name="w_column")
 
-        nc.scalar.dma_start(w_column[:], w)
-        nc.sync.dma_start(wk_heads[0][:], wk_view[:, :, 0:P])
-        nc.sync.dma_start(x_pieces[0][:], x_view[:, :, 0:PIECE])
-        nc.sync.dma_start(offsets[:], offs)
-        nc.sync.dma_start(windows[0][:], base[0:P, :])
-        nc.sync.dma_start(wk_heads[1][:], wk_view[:, :, P : 2 * P])
-        nc.sync.dma_start(windows[1][:], base[P : 2 * P, :])
-        for t in range(1, PIECES):
-            nc.sync.dma_start(x_pieces[t][:], x_view[:, :, t * PIECE : (t + 1) * PIECE])
-        for h in range(PAIR, HEADS):
+        def load_x(first_token, tokens):
+            columns = slice(first_token, first_token + tokens)
+            nc.sync.dma_start(x_all[:, :, columns], x_view[:, :, columns])
+
+        def load_wk(h):
             nc.sync.dma_start(wk_heads[h][:], wk_view[:, :, h * P : (h + 1) * P])
-        for h in range(PAIR, HEADS):
+
+        def load_window(h):
             nc.sync.dma_start(windows[h][:], base[h * P : (h + 1) * P, :])
+
+        nc.scalar.dma_start(w_column[:], w)
+        load_wk(0)
+        load_x(0, PIECE)
+        load_wk(1)
+        nc.sync.dma_start(offsets[:], offs)
+        load_window(0)
+        load_x(PIECE, PIECE)
+        load_window(1)
+        for h in range(PAIR, HEADS):
+            load_wk(h)
+            load_window(h)
 
         eps = held.tile([P, 1], F32, name="eps")
         nc.vector.memset(eps[:], EPS)
@@ -65,18 +72,16 @@ def tile_fullattention_kernel(tc, x, wk, w, base, offs, out):
         gain = held.tile([P, 1], F32, name="gain")
         nc.vector.tensor_scalar_add(gain[:], w_column[:], 1.0)
 
-        def project_normalise_scatter(h, first_piece, pieces):
-            tokens = pieces * PIECE
+        def project_normalise_scatter(h, first_token, tokens):
             kp = kp_banks.tile([P, TOKENS], F32, name="kp")
-            for i in range(pieces):
-                for k in range(HID_BLOCKS):
-                    nc.tensor.matmul(
-                        kp[:, i * PIECE : (i + 1) * PIECE],
-                        wk_heads[h][:, k, :],
-                        x_pieces[first_piece + i][:, k, :],
-                        start=(k == 0),
-                        stop=(k == HID_BLOCKS - 1),
-                    )
+            for k in range(HID_BLOCKS):
+                nc.tensor.matmul(
+                    kp[:, 0:tokens],
+                    wk_heads[h][:, k, :],
+                    x_all[:, k, first_token : first_token + tokens],
+                    start=(k == 0),
+                    stop=(k == HID_BLOCKS - 1),
+                )
             squares = work.tile([P, TOKENS], BF16, name="squares")
             nc.scalar.activation(squares[:, 0:tokens], kp[:, 0:tokens], ACT.Square)
             mean_square = mean_banks.tile([P, TOKENS], F32, name="mean_square")
@@ -86,15 +91,18 @@ def tile_fullattention_kernel(tc, x, wk, w, base, offs, out):
             r = work.tile([P, TOKENS], F32, name="r")
             nc.scalar.activation(r[:, 0:tokens], mean_square[:, 0:tokens], ACT.Abs_reciprocal_sqrt, bias=eps[:])
 
-            first_column = first_piece * PIECE // 16
-            piece_offsets = offsets[:, first_column : first_column + tokens // 16]
+            piece_offsets = offsets[:, first_token // 16 : (first_token + tokens) // 16]
             nc.vector.tensor_tensor(windows[h][:].indirect(piece_offsets), gained[:, 0:tokens], r[:, 0:tokens], MULT)
 
-        for t in range(PIECES):
-            for h in range(PAIR):
-                project_normalise_scatter(h, t, 1)
+        def store_window(h):
+            nc.sync.dma_start(out[h * P : (h + 1) * P, :], windows[h][:])
+
+        for first_token in (0, PIECE // 2):
+            project_normalise_scatter(0, first_token, PIECE // 2)
+        project_normalise_scatter(1, 0, PIECE)
         for h in range(PAIR):
-            nc.sync.dma_start(out[h * P : (h + 1) * P, :], windows[h][:])
+            project_normalise_scatter(h, PIECE, PIECE)
+            store_window(h)
         for h in range(PAIR, HEADS):
-            project_normalise_scatter(h, 0, PIECES)
-            nc.sync.dma_start(out[h * P : (h + 1) * P, :], windows[h][:])
+            project_normalise_scatter(h, 0, TOKENS)
+            store_window(h)

@@ -30,7 +30,7 @@ def tile_fullattention_kernel(tc, x, wk, w, base, offs, out):
         tc.psum_pool(name="idle_banks", bufs=1) as idle_banks,
     ):
         x_all = held.tile([P, HID_BLOCKS, TOKENS], BF16, name="x_all")
-        wk_heads = [held.tile([P, HID_BLOCKS, P], BF16, name=f"wk_head{h}") for h in range(HEADS)]
+        wk_pairs = [held.tile([P, HID_BLOCKS, PAIR * P], BF16, name=f"wk_pair{i}") for i in range(HEADS // PAIR)]
         windows = [held.tile([P, PLACES], F32, name=f"window{h}") for h in range(HEADS)]
         offsets = held.tile([P, TOKENS // 16], U16, name="offsets")
         w_column = held.tile([P, 1], F32, name="w_column")
@@ -39,22 +39,21 @@ def tile_fullattention_kernel(tc, x, wk, w, base, offs, out):
             columns = slice(first_token, first_token + tokens)
             nc.sync.dma_start(x_all[:, :, columns], x_view[:, :, columns])
 
-        def load_wk(h):
-            nc.sync.dma_start(wk_heads[h][:], wk_view[:, :, h * P : (h + 1) * P])
+        def load_wk_pair(i):
+            nc.sync.dma_start(wk_pairs[i][:], wk_view[:, :, i * PAIR * P : (i + 1) * PAIR * P])
 
         def load_window(h):
             nc.sync.dma_start(windows[h][:], base[h * P : (h + 1) * P, :])
 
         nc.scalar.dma_start(w_column[:], w)
-        load_wk(0)
+        load_wk_pair(0)
         load_x(0, PIECE)
-        load_wk(1)
         nc.sync.dma_start(offsets[:], offs)
         load_window(0)
         load_x(PIECE, PIECE)
         load_window(1)
+        load_wk_pair(1)
         for h in range(PAIR, HEADS):
-            load_wk(h)
             load_window(h)
 
         eps = held.tile([P, 1], F32, name="eps")
@@ -77,7 +76,7 @@ def tile_fullattention_kernel(tc, x, wk, w, base, offs, out):
             for k in range(HID_BLOCKS):
                 nc.tensor.matmul(
                     kp[:, 0:tokens],
-                    wk_heads[h][:, k, :],
+                    wk_pairs[h // PAIR][:, k, (h % PAIR) * P : (h % PAIR + 1) * P],
                     x_all[:, k, first_token : first_token + tokens],
                     start=(k == 0),
                     stop=(k == HID_BLOCKS - 1),

@@ -45,9 +45,9 @@ def tile_fullattention_kernel(tc, x, wk, w, base, offs, out):
         def load_window(h):
             nc.sync.dma_start(windows[h][:], base[h * P : (h + 1) * P, :])
 
+        nc.scalar.dma_start(x_all[:, :, 0:PIECE], x_view[:, :, 0:PIECE])
         nc.scalar.dma_start(w_column[:], w)
         load_wk_pair(0)
-        load_x(0, PIECE)
         nc.sync.dma_start(offsets[:], offs)
         load_window(0)
         load_x(PIECE, PIECE)

@@ -71,7 +71,7 @@ def tile_fullattention_kernel(tc, x, wk, w, base, offs, out):
         gain = held.tile([P, 1], F32, name="gain")
         nc.vector.tensor_scalar_add(gain[:], w_column[:], 1.0)
 
-        def project_normalise_scatter(h, first_token, tokens):
+        def project_normalise_scatter(h, first_token, tokens, gain_on_vector=False):
             kp = kp_banks.tile([P, TOKENS], F32, name="kp")
             for k in range(HID_BLOCKS):
                 nc.tensor.matmul(
@@ -86,7 +86,10 @@ def tile_fullattention_kernel(tc, x, wk, w, base, offs, out):
             mean_square = mean_banks.tile([P, TOKENS], F32, name="mean_square")
             nc.tensor.matmul(mean_square[:, 0:tokens], averager, squares[:, 0:tokens], start=True, stop=True)
             gained = work.tile([P, TOKENS], F32, name="gained")
-            nc.scalar.activation(gained[:, 0:tokens], kp[:, 0:tokens], ACT.Identity, scale=gain[:])
+            if gain_on_vector:
+                nc.vector.tensor_scalar_mul(gained[:, 0:tokens], kp[:, 0:tokens], gain[:])
+            else:
+                nc.scalar.activation(gained[:, 0:tokens], kp[:, 0:tokens], ACT.Identity, scale=gain[:])
             r = work.tile([P, TOKENS], F32, name="r")
             nc.scalar.activation(r[:, 0:tokens], mean_square[:, 0:tokens], ACT.Abs_reciprocal_sqrt, bias=eps[:])
 
@@ -97,7 +100,7 @@ def tile_fullattention_kernel(tc, x, wk, w, base, offs, out):
             nc.sync.dma_start(out[h * P : (h + 1) * P, :], windows[h][:])
 
         for first_token in (0, PIECE // 2):
-            project_normalise_scatter(0, first_token, PIECE // 2)
+            project_normalise_scatter(0, first_token, PIECE // 2, gain_on_vector=True)
         project_normalise_scatter(1, 0, PIECE)
         for h in range(PAIR):
             project_normalise_scatter(h, PIECE, PIECE)

import concourse.mybir as mybir

BF16, F32, U16 = mybir.dt.bfloat16, mybir.dt.float32, mybir.dt.uint16
ACT = mybir.ActivationFunctionType
MULT = mybir.AluOpType.mult

P = 128
HID = 512
HEADS = 4
TOKENS = 512
PLACES = 1024
HID_BLOCKS = HID // P
EPS = 1e-6
PAIR = 2
PIECE = 256
PE_WARMERS = 4

FLOPS = 2 * HID * HEADS * P * TOKENS


def tile_fullattention_kernel(tc, x, wk, w, base, offs, out):
    nc = tc.nc
    x_view = x.rearrange("(k p) j -> p k j", p=P)
    wk_view = wk.rearrange("(k p) c -> p k c", p=P)
    with (
        tc.tile_pool(name="held", bufs=1) as held,
        tc.tile_pool(name="work", bufs=3) as work,
        tc.psum_pool(name="kp_banks", bufs=3) as kp_banks,
        tc.psum_pool(name="mean_banks", bufs=2) as mean_banks,
        tc.psum_pool(name="idle_banks", bufs=1) as idle_banks,
    ):
        x_all = held.tile([P, HID_BLOCKS, TOKENS], BF16, name="x_all")
        wk_pairs = [held.tile([P, HID_BLOCKS, PAIR * P], BF16, name=f"wk_pair{i}") for i in range(HEADS // PAIR)]
        windows = [held.tile([P, PLACES], F32, name=f"window{h}") for h in range(HEADS)]
        offsets = held.tile([P, TOKENS // 16], U16, name="offsets")
        w_column = held.tile([P, 1], F32, name="w_column")

        def load_x(first_token, tokens):
            columns = slice(first_token, first_token + tokens)
            nc.sync.dma_start(x_all[:, :, columns], x_view[:, :, columns])

        def load_wk_pair(i):
            nc.sync.dma_start(wk_pairs[i][:], wk_view[:, :, i * PAIR * P : (i + 1) * PAIR * P])

        def load_window(h):
            nc.sync.dma_start(windows[h][:], base[h * P : (h + 1) * P, :])

        nc.scalar.dma_start(x_all[:, :, 0:PIECE], x_view[:, :, 0:PIECE])
        nc.scalar.dma_start(w_column[:], w)
        load_wk_pair(0)
        nc.sync.dma_start(offsets[:], offs)
        load_window(0)
        load_x(PIECE, PIECE)
        load_window(1)
        load_wk_pair(1)
        for h in range(PAIR, HEADS):
            load_window(h)

        eps = held.tile([P, 1], F32, name="eps")
        nc.vector.memset(eps[:], EPS)
        table_warmer = held.tile([P, 1], F32, name="table_warmer")
        nc.scalar.activation(table_warmer[:], eps[:], ACT.Abs_reciprocal_sqrt)
        fractions = held.tile([P, TOKENS], BF16, name="fractions")
        nc.vector.memset(fractions[:], 1.0 / P)
        averager = fractions[:, 0:P]

        idle_product = idle_banks.tile([P, TOKENS], F32, name="idle_product")
        for i in range(PE_WARMERS):
            nc.tensor.matmul(idle_product[:], averager, fractions[:], start=True, stop=True)

        gain = held.tile([P, 1], F32, name="gain")
        nc.vector.tensor_scalar_add(gain[:], w_column[:], 1.0)

        def project_normalise_scatter(h, first_token, tokens, gain_on_vector=False):
            kp = kp_banks.tile([P, TOKENS], F32, name="kp")
            for k in range(HID_BLOCKS):
                nc.tensor.matmul(
                    kp[:, 0:tokens],
                    wk_pairs[h // PAIR][:, k, (h % PAIR) * P : (h % PAIR + 1) * P],
                    x_all[:, k, first_token : first_token + tokens],
                    start=(k == 0),
                    stop=(k == HID_BLOCKS - 1),
                )
            squares = work.tile([P, TOKENS], BF16, name="squares")
            nc.scalar.activation(squares[:, 0:tokens], kp[:, 0:tokens], ACT.Square)
            mean_square = mean_banks.tile([P, TOKENS], F32, name="mean_square")
            nc.tensor.matmul(mean_square[:, 0:tokens], averager, squares[:, 0:tokens], start=True, stop=True)
            gained = work.tile([P, TOKENS], F32, name="gained")
            if gain_on_vector:
                nc.vector.tensor_scalar_mul(gained[:, 0:tokens], kp[:, 0:tokens], gain[:])
            else:
                nc.scalar.activation(gained[:, 0:tokens], kp[:, 0:tokens], ACT.Identity, scale=gain[:])
            r = work.tile([P, TOKENS], F32, name="r")
            nc.scalar.activation(r[:, 0:tokens], mean_square[:, 0:tokens], ACT.Abs_reciprocal_sqrt, bias=eps[:])

            piece_offsets = offsets[:, first_token // 16 : (first_token + tokens) // 16]
            nc.vector.tensor_tensor(windows[h][:].indirect(piece_offsets), gained[:, 0:tokens], r[:, 0:tokens], MULT)

        def store_window(h):
            nc.sync.dma_start(out[h * P : (h + 1) * P, :], windows[h][:])

        for first_token in (0, PIECE // 2):
            project_normalise_scatter(0, first_token, PIECE // 2, gain_on_vector=True)
        project_normalise_scatter(1, 0, PIECE)
        for h in range(PAIR):
            project_normalise_scatter(h, PIECE, PIECE)
            store_window(h)
        for h in range(PAIR, HEADS):
            project_normalise_scatter(h, 0, TOKENS)
            store_window(h)
